import numpy as np
import ml_dtypes


def mxq(x, axis, fmt="e4m3"):
    dtype, down = {"e4m3": (ml_dtypes.float8_e4m3fn, 7), "e5m2": (ml_dtypes.float8_e5m2, 14)}[fmt]
    v = np.moveaxis(np.asarray(x, np.float32).astype(ml_dtypes.bfloat16).astype(np.float64), axis, -1)
    blocks = v.reshape(v.shape[:-1] + (-1, 32))
    amax = np.abs(blocks).max(-1, keepdims=True)
    byte = np.maximum(np.where(amax > 0, np.frexp(amax)[1] - 1 + 127, 0) - down, 1)
    scale = np.exp2(byte - 127.0)
    codes = (blocks / scale).astype(np.float32).astype(dtype).astype(np.float64)
    return np.moveaxis((codes * scale).reshape(v.shape), -1, axis)


WIDE = False


def mx_kscale(k):
    if not WIDE:
        return np.ones(k)
    levels = np.array([10, -10, 5, -5, 0])
    a = np.random.permutation(np.resize(levels, k // 512 * 4)).reshape(k // 512, 4)
    idx = np.arange(k)
    return np.exp2(a[idx // 512, idx % 128 // 32])


BF16 = ml_dtypes.bfloat16


def bf(x):
    return np.asarray(x, np.float32).astype(BF16)


def f64(x):
    return np.asarray(x).astype(np.float64)


E2M1 = np.array([0.0, 0.5, 1.0, 1.5, 2.0, 3.0, 4.0, 6.0, -0.0, -0.5, -1.0, -1.5, -2.0, -3.0, -4.0, -6.0])


def pack_weight(w, fmt):
    k, n = w.shape
    w = f64(bf(w)).reshape(k // 32, 32, n)
    amax = np.abs(w).max(1)
    if fmt == "e4m3":
        byte = np.frexp(amax)[1] - 1 + 127 - 7
    else:
        mant, ex = np.frexp(amax / 6.0)
        byte = np.where(mant > 0.5, ex, ex - 1) + 127
    byte = np.clip(np.where(amax > 0, byte, 1), 1, 254)
    scaled = (w * np.exp2(127.0 - byte)[:, None, :]).reshape(k, n).astype(np.float32)
    by_word = np.ascontiguousarray(scaled.reshape(k // 512, 128, 4, n).transpose(0, 1, 3, 2))
    if fmt == "e4m3":
        words = by_word.astype(ml_dtypes.float8_e4m3fn).view(np.uint8)
    else:
        c = by_word.astype(ml_dtypes.float4_e2m1fn).view(np.uint8) & 0xF
        words = c[..., 0::2] | (c[..., 1::2] << 4)
    return np.ascontiguousarray(words), np.ascontiguousarray(byte.astype(np.uint8).reshape(k // 512, 16, n))


def unpack_weight(words, scales, fmt):
    g, p, n, _ = words.shape
    if fmt == "e4m3":
        vals = np.ascontiguousarray(words).view(ml_dtypes.float8_e4m3fn).astype(np.float64)
    else:
        nib = np.empty((g, p, n, 4), np.uint8)
        nib[..., 0::2] = words & 0xF
        nib[..., 1::2] = words >> 4
        vals = E2M1[nib]
    vals = vals * np.repeat(np.exp2(scales.astype(np.float64) - 127.0), 8, axis=1)[..., None]
    return vals.transpose(0, 1, 3, 2).reshape(g * 512, n)


B, IN, H, OUT, DEG = 512, 4096, 256, 512, 4


def cheby(t):
    ts = [np.ones_like(t), t]
    for _ in range(DEG - 1):
        ts.append(2.0 * t * ts[-1] - ts[-2])
    return np.concatenate(ts[1:], axis=-1)


def setup_inputs():
    s = mx_kscale(IN)
    r = np.random.standard_normal
    x = bf(r((B, IN)) * s)
    w1 = r((H, IN)) / np.sqrt(IN) / s
    words, scales = pack_weight(np.ascontiguousarray(w1.T), "e4m3")
    return {"x": x,
            "w1_base_words": words,
            "w1_base_scales": scales,
            "b1_base": bf(0.2 * r(H)),
            "c1": bf(r((IN, H, DEG + 1)) * 0.5 / np.sqrt(IN)),
            "s1": bf(1.0 + 0.1 * r(H))}


def reference(x, w1_base_words, w1_base_scales, b1_base, c1, s1):
    x, c = f64(x), f64(c1)
    base = (mxq(x, 1, "e4m3") @ unpack_weight(w1_base_words, w1_base_scales, "e4m3")) + f64(b1_base)
    tcat = cheby(np.tanh(x))
    ccat = c[:, :, 1:].transpose(2, 0, 1).reshape(DEG * IN, H)
    poly = c[:, :, 0].sum(0) + (mxq(tcat, 1, "e4m3") @ mxq(ccat, 0, "e4m3"))
    return base + poly * f64(s1)

@@ -1,0 +1,304 @@
+from contextlib import ExitStack
+
+import concourse.mybir as mybir
+from concourse.masks import make_identity
+
+F32 = mybir.dt.float32
+BF16 = mybir.dt.bfloat16
+I32 = mybir.dt.int32
+U32 = mybir.dt.uint32
+U8 = mybir.dt.uint8
+FP8X4 = mybir.dt.float8_e4m3fn_x4
+FUNC = mybir.ActivationFunctionType
+ALU = mybir.AluOpType
+
+ROWS, INPUTS, OUTPUTS, DEGREES = 512, 4096, 256, 4
+
+P = 128
+PACK = 4
+K_PASS = P * PACK
+PASSES = INPUTS // K_PASS
+ROW_TILES = ROWS // P
+
+CHUNK_PASSES = 4
+CHUNK_K = CHUNK_PASSES * K_PASS
+CHUNK_WORDS = CHUNK_PASSES * P
+CHUNKS_PER_ROW_TILE = PASSES // CHUNK_PASSES
+CHUNKS = ROW_TILES * CHUNKS_PER_ROW_TILE
+PAIR_WORDS = K_PASS // 2
+
+C_PAIRS = PASSES // 2
+C_LOADS_AHEAD = 3
+X_LOADS_AHEAD = 3
+
+FLOPS = 2 * ROWS * OUTPUTS * INPUTS * (DEGREES + 1)
+
+
+def tile_chebykanprojector_pa_k_kernel(
+    tc, x, w1_base_words, w1_base_scales, b1_base, c1, s1, out
+):
+    nc = tc.nc
+    with ExitStack() as ctx:
+        keep = ctx.enter_context(tc.tile_pool(name="keep", bufs=1))
+        x_pool = ctx.enter_context(tc.tile_pool(name="x_raw", bufs=X_LOADS_AHEAD + 1))
+        c_raw_pool = ctx.enter_context(tc.tile_pool(name="c_raw", bufs=C_LOADS_AHEAD))
+        c_grouped_pool = ctx.enter_context(tc.tile_pool(name="c_grouped", bufs=3))
+        work = ctx.enter_context(tc.tile_pool(name="work", bufs=2))
+        basis_pool = ctx.enter_context(tc.tile_pool(name="basis", bufs=1))
+        packed = ctx.enter_context(tc.tile_pool(name="packed", bufs=2))
+        result = ctx.enter_context(tc.tile_pool(name="result", bufs=2))
+        psum_x = ctx.enter_context(tc.psum_pool(name="psum_x", bufs=3))
+        psum_base = ctx.enter_context(tc.psum_pool(name="psum_base", bufs=2))
+        psum_poly = ctx.enter_context(tc.psum_pool(name="psum_poly", bufs=2))
+        psum_c0 = ctx.enter_context(tc.psum_pool(name="psum_c0", bufs=1))
+
+        identity = keep.tile([P, P], F32, name="identity")
+        ones = keep.tile([P, P], BF16, name="ones")
+        w_codes = keep.tile([P, PASSES, OUTPUTS], U32, name="w_codes", align_bytes=64)
+        w_scales = keep.tile([P, PASSES, OUTPUTS], U8, name="w_scales", align_bytes=64)
+        c_codes = keep.tile([P, PASSES, DEGREES * OUTPUTS], U32, name="c_codes", align_bytes=64)
+        c_scales = keep.tile([P, PASSES, DEGREES * OUTPUTS], U8, name="c_scales", align_bytes=64)
+        gain_rows = keep.tile([P, OUTPUTS], BF16, name="gain_rows")
+        bias_rows = keep.tile([P, OUTPUTS], BF16, name="bias_rows")
+        offset_rows = keep.tile([P, OUTPUTS], F32, name="offset_rows")
+        c0_sum = psum_c0.tile([P, OUTPUTS], F32, name="c0_sum")
+
+        x_raw, x_banks, x_grouped = {}, {}, {}
+        tanh_x, four_t_sq, t2_sq = {}, {}, {}
+        basis, operand = {}, {}
+        c_raw, c_grouped = {}, {}
+        base_acc, poly_acc = {}, {}
+
+        def is_chunk(s):
+            return 0 <= s < CHUNKS
+
+        def load_x(s):
+            if not is_chunk(s):
+                return
+            rows = slice((s // CHUNKS_PER_ROW_TILE) * P, (s // CHUNKS_PER_ROW_TILE + 1) * P)
+            cols = slice((s % CHUNKS_PER_ROW_TILE) * CHUNK_K, (s % CHUNKS_PER_ROW_TILE + 1) * CHUNK_K)
+            x_raw[s] = x_pool.tile([P, CHUNK_K], BF16, name="x_raw", tag="x_raw")
+            nc.sync.dma_start(out=x_raw[s][:], in_=x[rows, cols])
+
+        def load_c(g):
+            if g >= PASSES:
+                return
+            c_raw[g] = c_raw_pool.tile([P, PACK, OUTPUTS, DEGREES + 1], BF16, name="c_raw", tag="c_raw")
+            nc.sync.dma_start(
+                out=c_raw[g][:],
+                in_=c1[g * K_PASS : (g + 1) * K_PASS].rearrange("(p j) o e -> p j o e", j=PACK),
+            )
+
+        def load_w():
+            nc.vector.memset(w_scales[:].bitcast(I32), 0)
+            scale_rows = w1_base_scales.rearrange("g q n -> q g n")
+            for quadrant in range(4):
+                nc.sync.dma_start(
+                    out=w_scales[32 * quadrant : 32 * quadrant + 4].bitcast(I32),
+                    in_=scale_rows[4 * quadrant : 4 * quadrant + 4].bitcast(I32),
+                )
+            nc.sync.dma_start(
+                out=w_codes[:].bitcast(I32),
+                in_=w1_base_words.rearrange("g p n t -> p g (n t)").bitcast(I32),
+            )
+
+        def transpose_x(s):
+            if not is_chunk(s):
+                return
+            words = x_raw[s][:].bitcast(F32)
+            x_banks[s] = []
+            for half in range(CHUNK_PASSES // 2):
+                bank = psum_x.tile([P, 2, 2, P], F32, name="x_bank", tag="x_bank")
+                for g in range(2):
+                    first = (2 * half + g) * PAIR_WORDS
+                    for u in range(2):
+                        nc.tensor.transpose(
+                            bank[:, g, u, :], words[:, first + u : first + PAIR_WORDS : 2], identity[:]
+                        )
+                x_banks[s].append(bank)
+
+        def copy_x(s):
+            if not is_chunk(s):
+                return
+            x_grouped[s] = work.tile([P, CHUNK_WORDS * PACK], BF16, name="x_grouped", tag="x_grouped", align_bytes=64)
+            words = x_grouped[s][:].bitcast(F32).rearrange("p (g r u) -> p g r u", g=CHUNK_PASSES, u=2)
+            for half in range(CHUNK_PASSES // 2):
+                nc.scalar.copy(
+                    out=words[:, 2 * half : 2 * half + 2],
+                    in_=x_banks[s][half][:].rearrange("p g u r -> p g r u"),
+                )
+
+        def float_tile(name):
+            return work.tile([P, CHUNK_WORDS * PACK], F32, name=name, tag=name)
+
+        def tanh_of_x(s):
+            if not is_chunk(s):
+                return
+            tanh_x[s] = float_tile("tanh_x")
+            nc.scalar.activation(out=tanh_x[s][:], in_=x_grouped[s][:], func=FUNC.Tanh)
+
+        def square_twice_t(s):
+            if not is_chunk(s):
+                return
+            four_t_sq[s] = float_tile("four_t_sq")
+            nc.scalar.activation(out=four_t_sq[s][:], in_=tanh_x[s][:], func=FUNC.Square, scale=2.0)
+
+        def square_t2(s):
+            if not is_chunk(s):
+                return
+            t2_sq[s] = float_tile("t2_sq")
+            nc.scalar.activation(out=t2_sq[s][:], in_=four_t_sq[s][:], func=FUNC.Square, scale=0.5, bias=-1.0)
+
+        def basis_tile(s, d):
+            name = "basis_%d" % d
+            basis[s, d] = basis_pool.tile([P, CHUNK_WORDS * PACK], BF16, name=name, tag=name, align_bytes=64)
+            return basis[s, d]
+
+        def degree_1(s):
+            if is_chunk(s):
+                nc.vector.tensor_copy(out=basis_tile(s, 1)[:], in_=tanh_x[s][:])
+
+        def degree_2(s):
+            if is_chunk(s):
+                nc.vector.tensor_scalar(
+                    out=basis_tile(s, 2)[:], in0=four_t_sq[s][:], scalar1=0.5, scalar2=-1.0, op0=ALU.mult, op1=ALU.add
+                )
+
+        def degree_3(s):
+            if is_chunk(s):
+                nc.vector.scalar_tensor_tensor(
+                    out=basis_tile(s, 3)[:], in0=four_t_sq[s][:], scalar=3.0, in1=tanh_x[s][:],
+                    op0=ALU.subtract, op1=ALU.mult,
+                )
+
+        def degree_4(s):
+            if is_chunk(s):
+                nc.vector.tensor_scalar(
+                    out=basis_tile(s, 4)[:], in0=t2_sq[s][:], scalar1=2.0, scalar2=-1.0, op0=ALU.mult, op1=ALU.add
+                )
+
+        def quantise(s, d):
+            if not is_chunk(s):
+                return
+            values = x_grouped[s] if d == 0 else basis[s, d]
+            codes = packed.tile([P, CHUNK_WORDS], U32, name="codes_%d" % d, tag="codes_%d" % d, align_bytes=64)
+            scales = packed.tile([P, CHUNK_WORDS], U8, name="scales_%d" % d, tag="scales_%d" % d, align_bytes=64)
+            nc.vector.quantize_mx(out=codes[:].bitcast(FP8X4), scales=scales[:], in_=values[:])
+            operand[s, d] = (codes, scales)
+
+        def regroup_c_pair(k):
+            if not 0 <= k < C_PAIRS:
+                return
+            for g in (2 * k, 2 * k + 1):
+                c_grouped[g] = c_grouped_pool.tile(
+                    [P, DEGREES, OUTPUTS, PACK], BF16, name="c_grouped", tag="c_grouped", align_bytes=64
+                )
+                by_degree = c_raw[g][:, :, :, 1:].rearrange("p j o e -> p e o j")
+                if g % 2 == 0:
+                    nc.vector.tensor_copy(out=c_grouped[g][:], in_=by_degree)
+                else:
+                    nc.scalar.copy(out=c_grouped[g][:], in_=by_degree)
+                for j in range(PACK):
+                    nc.tensor.matmul(
+                        out=c0_sum[:], lhsT=ones[:], rhs=c_raw[g][:, j, :, 0],
+                        start=(g == 0 and j == 0), stop=(g == PASSES - 1 and j == PACK - 1),
+                    )
+            for g in (2 * k, 2 * k + 1):
+                load_c(g + C_LOADS_AHEAD)
+
+        def quantise_c_pair(k):
+            if not 0 <= k < C_PAIRS:
+                return
+            for g in (2 * k, 2 * k + 1):
+                nc.vector.quantize_mx(
+                    out=c_codes[:, g, :].bitcast(FP8X4),
+                    scales=c_scales[:, g, :],
+                    in_=c_grouped[g][:].rearrange("p e o j -> p (e o j)"),
+                )
+
+        def multiply(s, d):
+            if not is_chunk(s):
+                return
+            row_tile, part = s // CHUNKS_PER_ROW_TILE, s % CHUNKS_PER_ROW_TILE
+            first_part, last_part = part == 0, part == CHUNKS_PER_ROW_TILE - 1
+            if d == 0:
+                if first_part:
+                    base_acc[row_tile] = psum_base.tile([P, OUTPUTS], F32, name="base_acc", tag="base_acc")
+                acc, opens, closes = base_acc[row_tile], first_part, last_part
+            else:
+                if first_part and d == 1:
+                    poly_acc[row_tile] = psum_poly.tile([P, OUTPUTS], F32, name="poly_acc", tag="poly_acc")
+                acc, opens, closes = poly_acc[row_tile], first_part and d == 1, last_part and d == DEGREES
+            codes, scales = operand[s, d]
+            for local in range(CHUNK_PASSES):
+                g = part * CHUNK_PASSES + local
+                rows = slice(local * P, (local + 1) * P)
+                if d == 0:
+                    rhs, rhs_scale = w_codes[:, g, :], w_scales[:, g, :]
+                else:
+                    outputs = slice((d - 1) * OUTPUTS, d * OUTPUTS)
+                    rhs, rhs_scale = c_codes[:, g, outputs], c_scales[:, g, outputs]
+                nc.tensor.matmul_mx(
+                    out=acc[:],
+                    lhsT=codes[:, rows].bitcast(FP8X4),
+                    lhsT_scale=scales[:, rows],
+                    rhs=rhs.bitcast(FP8X4),
+                    rhs_scale=rhs_scale,
+                    start=(opens and local == 0),
+                    stop=(closes and local == CHUNK_PASSES - 1),
+                )
+
+        def make_offset_rows():
+            nc.vector.tensor_tensor(out=offset_rows[:], in0=c0_sum[:], in1=gain_rows[:], op=ALU.mult)
+            nc.vector.tensor_tensor(out=offset_rows[:], in0=offset_rows[:], in1=bias_rows[:], op=ALU.add)
+
+        def finish_rows(row_tile):
+            shifted = result.tile([P, OUTPUTS], F32, name="shifted", tag="shifted")
+            nc.vector.tensor_tensor(out=shifted[:], in0=base_acc[row_tile][:], in1=offset_rows[:], op=ALU.add)
+            scaled = result.tile([P, OUTPUTS], F32, name="scaled", tag="scaled")
+            nc.vector.tensor_tensor(out=scaled[:], in0=poly_acc[row_tile][:], in1=gain_rows[:], op=ALU.mult)
+            total = result.tile([P, OUTPUTS], F32, name="total", tag="total")
+            nc.vector.tensor_tensor(out=total[:], in0=scaled[:], in1=shifted[:], op=ALU.add)
+            nc.sync.dma_start(out=out[row_tile * P : (row_tile + 1) * P, :], in_=total[:])
+
+        make_identity(nc, identity[:])
+        nc.gpsimd.memset(ones[:], 1.0)
+        load_x(0)
+        load_c(0)
+        load_x(1)
+        load_w()
+        load_c(1)
+        load_c(2)
+
+        for s in range(-1, CHUNKS + 2):
+            transpose_x(s + 1)
+            tanh_of_x(s)
+            degree_2(s - 1)
+            degree_3(s - 1)
+            quantise(s - 1, 2)
+            if s >= 3 and s % CHUNKS_PER_ROW_TILE == 1:
+                finish_rows((s - 3) // CHUNKS_PER_ROW_TILE)
+            regroup_c_pair(2 * s)
+            square_t2(s - 1)
+            degree_1(s)
+            quantise(s - 1, 3)
+            quantise_c_pair(2 * s)
+            copy_x(s + 1)
+            degree_4(s - 1)
+            quantise(s, 1)
+            regroup_c_pair(2 * s + 1)
+            square_twice_t(s)
+            quantise(s + 1, 0)
+            quantise(s - 1, 4)
+            quantise_c_pair(2 * s + 1)
+            if s == 1:
+                nc.sync.dma_start(out=gain_rows[:], in_=s1.partition_broadcast(P))
+                nc.sync.dma_start(out=bias_rows[:], in_=b1_base.partition_broadcast(P))
+            if s == 2:
+                make_offset_rows()
+            multiply(s - 1, 2)
+            multiply(s - 1, 3)
+            multiply(s, 1)
+            multiply(s + 1, 0)
+            multiply(s - 1, 4)
+            load_x(s + X_LOADS_AHEAD)

@@ -193,11 +193,12 @@ def tile_chebykanprojector_pa_k_kernel(
                 c_grouped[g] = c_grouped_pool.tile(
                     [P, DEGREES, OUTPUTS, PACK], BF16, name="c_grouped", tag="c_grouped", align_bytes=64
                 )
-                by_degree = c_raw[g][:, :, :, 1:].rearrange("p j o e -> p e o j")
+                source = c_raw[g][:, :, :, 1:].rearrange("p j o e -> p o e j")
+                target = c_grouped[g][:].rearrange("p e o j -> p o e j")
                 if g % 2 == 0:
-                    nc.vector.tensor_copy(out=c_grouped[g][:], in_=by_degree)
+                    nc.vector.tensor_copy(out=target, in_=source)
                 else:
-                    nc.scalar.copy(out=c_grouped[g][:], in_=by_degree)
+                    nc.scalar.copy(out=target, in_=source)
                 for j in range(PACK):
                     nc.tensor.matmul(
                         out=c0_sum[:], lhsT=ones[:], rhs=c_raw[g][:, j, :, 0],

@@ -27,6 +27,8 @@ CHUNKS_PER_ROW_TILE = PASSES // CHUNK_PASSES
 CHUNKS = ROW_TILES * CHUNKS_PER_ROW_TILE
 PAIR_WORDS = K_PASS // 2
 
+SCALAR_LAST_CHUNKS = 1
+
 C_PAIRS = PASSES // 2
 C_LOADS_AHEAD = 3
 X_LOADS_AHEAD = 3
@@ -154,15 +156,21 @@ def tile_chebykanprojector_pa_k_kernel(
             basis[s, d] = basis_pool.tile([P, CHUNK_WORDS * PACK], BF16, name=name, tag=name, align_bytes=64)
             return basis[s, d]
 
+        def scale_and_shift(s, d, values, scale, shift):
+            if s >= CHUNKS - SCALAR_LAST_CHUNKS:
+                nc.scalar.activation(out=basis_tile(s, d)[:], in_=values[:], func=FUNC.Identity, scale=scale, bias=shift)
+            else:
+                nc.vector.tensor_scalar(
+                    out=basis_tile(s, d)[:], in0=values[:], scalar1=scale, scalar2=shift, op0=ALU.mult, op1=ALU.add
+                )
+
         def degree_1(s):
             if is_chunk(s):
-                nc.vector.tensor_copy(out=basis_tile(s, 1)[:], in_=tanh_x[s][:])
+                scale_and_shift(s, 1, tanh_x[s], 1.0, 0.0)
 
         def degree_2(s):
             if is_chunk(s):
-                nc.vector.tensor_scalar(
-                    out=basis_tile(s, 2)[:], in0=four_t_sq[s][:], scalar1=0.5, scalar2=-1.0, op0=ALU.mult, op1=ALU.add
-                )
+                scale_and_shift(s, 2, four_t_sq[s], 0.5, -1.0)
 
         def degree_3(s):
             if is_chunk(s):
@@ -173,9 +181,7 @@ def tile_chebykanprojector_pa_k_kernel(
 
         def degree_4(s):
             if is_chunk(s):
-                nc.vector.tensor_scalar(
-                    out=basis_tile(s, 4)[:], in0=t2_sq[s][:], scalar1=2.0, scalar2=-1.0, op0=ALU.mult, op1=ALU.add
-                )
+                scale_and_shift(s, 4, t2_sq[s], 2.0, -1.0)
 
         def quantise(s, d):
             if not is_chunk(s):

@@ -20,14 +20,14 @@ K_PASS = P * PACK
 PASSES = INPUTS // K_PASS
 ROW_TILES = ROWS // P
 
-CHUNK_PASSES = 4
+CHUNK_PASSES = 2
 CHUNK_K = CHUNK_PASSES * K_PASS
 CHUNK_WORDS = CHUNK_PASSES * P
 CHUNKS_PER_ROW_TILE = PASSES // CHUNK_PASSES
 CHUNKS = ROW_TILES * CHUNKS_PER_ROW_TILE
 PAIR_WORDS = K_PASS // 2
 
-SCALAR_LAST_CHUNKS = 1
+SCALAR_LAST_CHUNKS = 2
 
 C_PAIRS = PASSES // 2
 C_LOADS_AHEAD = 3
@@ -45,7 +45,7 @@ def tile_chebykanprojector_pa_k_kernel(
         x_pool = ctx.enter_context(tc.tile_pool(name="x_raw", bufs=X_LOADS_AHEAD + 1))
         c_raw_pool = ctx.enter_context(tc.tile_pool(name="c_raw", bufs=C_LOADS_AHEAD))
         c_grouped_pool = ctx.enter_context(tc.tile_pool(name="c_grouped", bufs=3))
-        work = ctx.enter_context(tc.tile_pool(name="work", bufs=2))
+        work = ctx.enter_context(tc.tile_pool(name="work", bufs=3))
         basis_pool = ctx.enter_context(tc.tile_pool(name="basis", bufs=1))
         packed = ctx.enter_context(tc.tile_pool(name="packed", bufs=2))
         result = ctx.enter_context(tc.tile_pool(name="result", bufs=2))
@@ -283,25 +283,23 @@ def tile_chebykanprojector_pa_k_kernel(
             degree_2(s - 1)
             degree_3(s - 1)
             quantise(s - 1, 2)
-            if s >= 3 and s % CHUNKS_PER_ROW_TILE == 1:
-                finish_rows((s - 3) // CHUNKS_PER_ROW_TILE)
-            regroup_c_pair(2 * s)
+            if s > CHUNKS_PER_ROW_TILE and s % CHUNKS_PER_ROW_TILE == 1:
+                finish_rows((s - 1) // CHUNKS_PER_ROW_TILE - 1)
+            regroup_c_pair(s)
             square_t2(s - 1)
             degree_1(s)
             quantise(s - 1, 3)
-            quantise_c_pair(2 * s)
+            quantise_c_pair(s)
             copy_x(s + 1)
             degree_4(s - 1)
             quantise(s, 1)
-            regroup_c_pair(2 * s + 1)
             square_twice_t(s)
             quantise(s + 1, 0)
             quantise(s - 1, 4)
-            quantise_c_pair(2 * s + 1)
-            if s == 1:
+            if s == CHUNKS_PER_ROW_TILE - 1:
                 nc.sync.dma_start(out=gain_rows[:], in_=s1.partition_broadcast(P))
                 nc.sync.dma_start(out=bias_rows[:], in_=b1_base.partition_broadcast(P))
-            if s == 2:
+            if s == CHUNKS_PER_ROW_TILE:
                 make_offset_rows()
             multiply(s - 1, 2)
             multiply(s - 1, 3)

@@ -199,8 +199,8 @@ def tile_chebykanprojector_pa_k_kernel(
                 c_grouped[g] = c_grouped_pool.tile(
                     [P, DEGREES, OUTPUTS, PACK], BF16, name="c_grouped", tag="c_grouped", align_bytes=64
                 )
-                source = c_raw[g][:, :, :, 1:].rearrange("p j o e -> p o e j")
-                target = c_grouped[g][:].rearrange("p e o j -> p o e j")
+                source = c_raw[g][:, :, :, 1:].rearrange("p j o e -> p o j e")
+                target = c_grouped[g][:].rearrange("p e o j -> p o j e")
                 if g % 2 == 0:
                     nc.vector.tensor_copy(out=target, in_=source)
                 else:

@@ -31,6 +31,7 @@ SCALAR_LAST_CHUNKS = 2
 
 C_PAIRS = PASSES // 2
 C_LOADS_AHEAD = 3
+FIRST_C_PIECES = 4
 X_LOADS_AHEAD = 3
 
 FLOPS = 2 * ROWS * OUTPUTS * INPUTS * (DEGREES + 1)
@@ -45,9 +46,9 @@ def tile_chebykanprojector_pa_k_kernel(
         x_pool = ctx.enter_context(tc.tile_pool(name="x_raw", bufs=X_LOADS_AHEAD + 1))
         c_raw_pool = ctx.enter_context(tc.tile_pool(name="c_raw", bufs=C_LOADS_AHEAD))
         c_grouped_pool = ctx.enter_context(tc.tile_pool(name="c_grouped", bufs=3))
-        work = ctx.enter_context(tc.tile_pool(name="work", bufs=3))
-        basis_pool = ctx.enter_context(tc.tile_pool(name="basis", bufs=1))
-        packed = ctx.enter_context(tc.tile_pool(name="packed", bufs=2))
+        work = ctx.enter_context(tc.tile_pool(name="work", bufs=4))
+        basis_pool = ctx.enter_context(tc.tile_pool(name="basis", bufs=2))
+        packed = ctx.enter_context(tc.tile_pool(name="packed", bufs=3))
         result = ctx.enter_context(tc.tile_pool(name="result", bufs=2))
         psum_x = ctx.enter_context(tc.psum_pool(name="psum_x", bufs=3))
         psum_base = ctx.enter_context(tc.psum_pool(name="psum_base", bufs=2))
@@ -82,14 +83,18 @@ def tile_chebykanprojector_pa_k_kernel(
             x_raw[s] = x_pool.tile([P, CHUNK_K], BF16, name="x_raw", tag="x_raw")
             nc.sync.dma_start(out=x_raw[s][:], in_=x[rows, cols])
 
+        def c_pieces(g):
+            pieces = FIRST_C_PIECES if g == 0 else 1
+            width = OUTPUTS // pieces
+            return [slice(q * width, (q + 1) * width) for q in range(pieces)]
+
         def load_c(g):
             if g >= PASSES:
                 return
             c_raw[g] = c_raw_pool.tile([P, PACK, OUTPUTS, DEGREES + 1], BF16, name="c_raw", tag="c_raw")
-            nc.sync.dma_start(
-                out=c_raw[g][:],
-                in_=c1[g * K_PASS : (g + 1) * K_PASS].rearrange("(p j) o e -> p j o e", j=PACK),
-            )
+            rows = c1[g * K_PASS : (g + 1) * K_PASS].rearrange("(p j) o e -> p j o e", j=PACK)
+            for cols in c_pieces(g):
+                nc.sync.dma_start(out=c_raw[g][:, :, cols, :], in_=rows[:, :, cols, :])
 
         def load_w():
             nc.vector.memset(w_scales[:].bitcast(I32), 0)
@@ -199,12 +204,13 @@ def tile_chebykanprojector_pa_k_kernel(
                 c_grouped[g] = c_grouped_pool.tile(
                     [P, DEGREES, OUTPUTS, PACK], BF16, name="c_grouped", tag="c_grouped", align_bytes=64
                 )
-                source = c_raw[g][:, :, :, 1:].rearrange("p j o e -> p o j e")
-                target = c_grouped[g][:].rearrange("p e o j -> p o j e")
-                if g % 2 == 0:
-                    nc.vector.tensor_copy(out=target, in_=source)
-                else:
-                    nc.scalar.copy(out=target, in_=source)
+                for cols in c_pieces(g):
+                    source = c_raw[g][:, :, cols, 1:].rearrange("p j o e -> p o j e")
+                    target = c_grouped[g][:, :, cols, :].rearrange("p e o j -> p o j e")
+                    if g % 2 == 0:
+                        nc.vector.tensor_copy(out=target, in_=source)
+                    else:
+                        nc.scalar.copy(out=target, in_=source)
                 for j in range(PACK):
                     nc.tensor.matmul(
                         out=c0_sum[:], lhsT=ones[:], rhs=c_raw[g][:, j, :, 0],

@@ -275,10 +275,10 @@ def tile_chebykanprojector_pa_k_kernel(
             nc.sync.dma_start(out=out[row_tile * P : (row_tile + 1) * P, :], in_=total[:])
 
         make_identity(nc, identity[:])
-        nc.gpsimd.memset(ones[:], 1.0)
+        nc.vector.tensor_scalar(out=ones[:], in0=identity[:], scalar1=0.0, scalar2=1.0, op0=ALU.mult, op1=ALU.add)
         load_x(0)
-        load_c(0)
         load_x(1)
+        load_c(0)
         load_w()
         load_c(1)
         load_c(2)

from contextlib import ExitStack

import concourse.mybir as mybir
from concourse.masks import make_identity

F32 = mybir.dt.float32
BF16 = mybir.dt.bfloat16
I32 = mybir.dt.int32
U32 = mybir.dt.uint32
U8 = mybir.dt.uint8
FP8X4 = mybir.dt.float8_e4m3fn_x4
FUNC = mybir.ActivationFunctionType
ALU = mybir.AluOpType

ROWS, INPUTS, OUTPUTS, DEGREES = 512, 4096, 256, 4

P = 128
PACK = 4
K_PASS = P * PACK
PASSES = INPUTS // K_PASS
ROW_TILES = ROWS // P

CHUNK_PASSES = 2
CHUNK_K = CHUNK_PASSES * K_PASS
CHUNK_WORDS = CHUNK_PASSES * P
CHUNKS_PER_ROW_TILE = PASSES // CHUNK_PASSES
CHUNKS = ROW_TILES * CHUNKS_PER_ROW_TILE
PAIR_WORDS = K_PASS // 2

SCALAR_LAST_CHUNKS = 2

C_PAIRS = PASSES // 2
C_LOADS_AHEAD = 3
FIRST_C_PIECES = 4
X_LOADS_AHEAD = 3

FLOPS = 2 * ROWS * OUTPUTS * INPUTS * (DEGREES + 1)


def tile_chebykanprojector_pa_k_kernel(
    tc, x, w1_base_words, w1_base_scales, b1_base, c1, s1, out
):
    nc = tc.nc
    with ExitStack() as ctx:
        keep = ctx.enter_context(tc.tile_pool(name="keep", bufs=1))
        x_pool = ctx.enter_context(tc.tile_pool(name="x_raw", bufs=X_LOADS_AHEAD + 1))
        c_raw_pool = ctx.enter_context(tc.tile_pool(name="c_raw", bufs=C_LOADS_AHEAD))
        c_grouped_pool = ctx.enter_context(tc.tile_pool(name="c_grouped", bufs=3))
        work = ctx.enter_context(tc.tile_pool(name="work", bufs=4))
        basis_pool = ctx.enter_context(tc.tile_pool(name="basis", bufs=2))
        packed = ctx.enter_context(tc.tile_pool(name="packed", bufs=3))
        result = ctx.enter_context(tc.tile_pool(name="result", bufs=2))
        psum_x = ctx.enter_context(tc.psum_pool(name="psum_x", bufs=3))
        psum_base = ctx.enter_context(tc.psum_pool(name="psum_base", bufs=2))
        psum_poly = ctx.enter_context(tc.psum_pool(name="psum_poly", bufs=2))
        psum_c0 = ctx.enter_context(tc.psum_pool(name="psum_c0", bufs=1))

        identity = keep.tile([P, P], F32, name="identity")
        ones = keep.tile([P, P], BF16, name="ones")
        w_codes = keep.tile([P, PASSES, OUTPUTS], U32, name="w_codes", align_bytes=64)
        w_scales = keep.tile([P, PASSES, OUTPUTS], U8, name="w_scales", align_bytes=64)
        c_codes = keep.tile([P, PASSES, DEGREES * OUTPUTS], U32, name="c_codes", align_bytes=64)
        c_scales = keep.tile([P, PASSES, DEGREES * OUTPUTS], U8, name="c_scales", align_bytes=64)
        gain_rows = keep.tile([P, OUTPUTS], BF16, name="gain_rows")
        bias_rows = keep.tile([P, OUTPUTS], BF16, name="bias_rows")
        offset_rows = keep.tile([P, OUTPUTS], F32, name="offset_rows")
        c0_sum = psum_c0.tile([P, OUTPUTS], F32, name="c0_sum")

        x_raw, x_banks, x_grouped = {}, {}, {}
        tanh_x, four_t_sq, t2_sq = {}, {}, {}
        basis, operand = {}, {}
        c_raw, c_grouped = {}, {}
        base_acc, poly_acc = {}, {}

        def is_chunk(s):
            return 0 <= s < CHUNKS

        def load_x(s):
            if not is_chunk(s):
                return
            rows = slice((s // CHUNKS_PER_ROW_TILE) * P, (s // CHUNKS_PER_ROW_TILE + 1) * P)
            cols = slice((s % CHUNKS_PER_ROW_TILE) * CHUNK_K, (s % CHUNKS_PER_ROW_TILE + 1) * CHUNK_K)
            x_raw[s] = x_pool.tile([P, CHUNK_K], BF16, name="x_raw", tag="x_raw")
            nc.sync.dma_start(out=x_raw[s][:], in_=x[rows, cols])

        def c_pieces(g):
            pieces = FIRST_C_PIECES if g == 0 else 1
            width = OUTPUTS // pieces
            return [slice(q * width, (q + 1) * width) for q in range(pieces)]

        def load_c(g):
            if g >= PASSES:
                return
            c_raw[g] = c_raw_pool.tile([P, PACK, OUTPUTS, DEGREES + 1], BF16, name="c_raw", tag="c_raw")
            rows = c1[g * K_PASS : (g + 1) * K_PASS].rearrange("(p j) o e -> p j o e", j=PACK)
            for cols in c_pieces(g):
                nc.sync.dma_start(out=c_raw[g][:, :, cols, :], in_=rows[:, :, cols, :])

        def load_w():
            nc.vector.memset(w_scales[:].bitcast(I32), 0)
            scale_rows = w1_base_scales.rearrange("g q n -> q g n")
            for quadrant in range(4):
                nc.sync.dma_start(
                    out=w_scales[32 * quadrant : 32 * quadrant + 4].bitcast(I32),
                    in_=scale_rows[4 * quadrant : 4 * quadrant + 4].bitcast(I32),
                )
            nc.sync.dma_start(
                out=w_codes[:].bitcast(I32),
                in_=w1_base_words.rearrange("g p n t -> p g (n t)").bitcast(I32),
            )

        def transpose_x(s):
            if not is_chunk(s):
                return
            words = x_raw[s][:].bitcast(F32)
            x_banks[s] = []
            for half in range(CHUNK_PASSES // 2):
                bank = psum_x.tile([P, 2, 2, P], F32, name="x_bank", tag="x_bank")
                for g in range(2):
                    first = (2 * half + g) * PAIR_WORDS
                    for u in range(2):
                        nc.tensor.transpose(
                            bank[:, g, u, :], words[:, first + u : first + PAIR_WORDS : 2], identity[:]
                        )
                x_banks[s].append(bank)

        def copy_x(s):
            if not is_chunk(s):
                return
            x_grouped[s] = work.tile([P, CHUNK_WORDS * PACK], BF16, name="x_grouped", tag="x_grouped", align_bytes=64)
            words = x_grouped[s][:].bitcast(F32).rearrange("p (g r u) -> p g r u", g=CHUNK_PASSES, u=2)
            for half in range(CHUNK_PASSES // 2):
                nc.scalar.copy(
                    out=words[:, 2 * half : 2 * half + 2],
                    in_=x_banks[s][half][:].rearrange("p g u r -> p g r u"),
                )

        def float_tile(name):
            return work.tile([P, CHUNK_WORDS * PACK], F32, name=name, tag=name)

        def tanh_of_x(s):
            if not is_chunk(s):
                return
            tanh_x[s] = float_tile("tanh_x")
            nc.scalar.activation(out=tanh_x[s][:], in_=x_grouped[s][:], func=FUNC.Tanh)

        def square_twice_t(s):
            if not is_chunk(s):
                return
            four_t_sq[s] = float_tile("four_t_sq")
            nc.scalar.activation(out=four_t_sq[s][:], in_=tanh_x[s][:], func=FUNC.Square, scale=2.0)

        def square_t2(s):
            if not is_chunk(s):
                return
            t2_sq[s] = float_tile("t2_sq")
            nc.scalar.activation(out=t2_sq[s][:], in_=four_t_sq[s][:], func=FUNC.Square, scale=0.5, bias=-1.0)

        def basis_tile(s, d):
            name = "basis_%d" % d
            basis[s, d] = basis_pool.tile([P, CHUNK_WORDS * PACK], BF16, name=name, tag=name, align_bytes=64)
            return basis[s, d]

        def scale_and_shift(s, d, values, scale, shift):
            if s >= CHUNKS - SCALAR_LAST_CHUNKS:
                nc.scalar.activation(out=basis_tile(s, d)[:], in_=values[:], func=FUNC.Identity, scale=scale, bias=shift)
            else:
                nc.vector.tensor_scalar(
                    out=basis_tile(s, d)[:], in0=values[:], scalar1=scale, scalar2=shift, op0=ALU.mult, op1=ALU.add
                )

        def degree_1(s):
            if is_chunk(s):
                scale_and_shift(s, 1, tanh_x[s], 1.0, 0.0)

        def degree_2(s):
            if is_chunk(s):
                scale_and_shift(s, 2, four_t_sq[s], 0.5, -1.0)

        def degree_3(s):
            if is_chunk(s):
                nc.vector.scalar_tensor_tensor(
                    out=basis_tile(s, 3)[:], in0=four_t_sq[s][:], scalar=3.0, in1=tanh_x[s][:],
                    op0=ALU.subtract, op1=ALU.mult,
                )

        def degree_4(s):
            if is_chunk(s):
                scale_and_shift(s, 4, t2_sq[s], 2.0, -1.0)

        def quantise(s, d):
            if not is_chunk(s):
                return
            values = x_grouped[s] if d == 0 else basis[s, d]
            codes = packed.tile([P, CHUNK_WORDS], U32, name="codes_%d" % d, tag="codes_%d" % d, align_bytes=64)
            scales = packed.tile([P, CHUNK_WORDS], U8, name="scales_%d" % d, tag="scales_%d" % d, align_bytes=64)
            nc.vector.quantize_mx(out=codes[:].bitcast(FP8X4), scales=scales[:], in_=values[:])
            operand[s, d] = (codes, scales)

        def regroup_c_pair(k):
            if not 0 <= k < C_PAIRS:
                return
            for g in (2 * k, 2 * k + 1):
                c_grouped[g] = c_grouped_pool.tile(
                    [P, DEGREES, OUTPUTS, PACK], BF16, name="c_grouped", tag="c_grouped", align_bytes=64
                )
                for cols in c_pieces(g):
                    source = c_raw[g][:, :, cols, 1:].rearrange("p j o e -> p o j e")
                    target = c_grouped[g][:, :, cols, :].rearrange("p e o j -> p o j e")
                    if g % 2 == 0:
                        nc.vector.tensor_copy(out=target, in_=source)
                    else:
                        nc.scalar.copy(out=target, in_=source)
                for j in range(PACK):
                    nc.tensor.matmul(
                        out=c0_sum[:], lhsT=ones[:], rhs=c_raw[g][:, j, :, 0],
                        start=(g == 0 and j == 0), stop=(g == PASSES - 1 and j == PACK - 1),
                    )
            for g in (2 * k, 2 * k + 1):
                load_c(g + C_LOADS_AHEAD)

        def quantise_c_pair(k):
            if not 0 <= k < C_PAIRS:
                return
            for g in (2 * k, 2 * k + 1):
                nc.vector.quantize_mx(
                    out=c_codes[:, g, :].bitcast(FP8X4),
                    scales=c_scales[:, g, :],
                    in_=c_grouped[g][:].rearrange("p e o j -> p (e o j)"),
                )

        def multiply(s, d):
            if not is_chunk(s):
                return
            row_tile, part = s // CHUNKS_PER_ROW_TILE, s % CHUNKS_PER_ROW_TILE
            first_part, last_part = part == 0, part == CHUNKS_PER_ROW_TILE - 1
            if d == 0:
                if first_part:
                    base_acc[row_tile] = psum_base.tile([P, OUTPUTS], F32, name="base_acc", tag="base_acc")
                acc, opens, closes = base_acc[row_tile], first_part, last_part
            else:
                if first_part and d == 1:
                    poly_acc[row_tile] = psum_poly.tile([P, OUTPUTS], F32, name="poly_acc", tag="poly_acc")
                acc, opens, closes = poly_acc[row_tile], first_part and d == 1, last_part and d == DEGREES
            codes, scales = operand[s, d]
            for local in range(CHUNK_PASSES):
                g = part * CHUNK_PASSES + local
                rows = slice(local * P, (local + 1) * P)
                if d == 0:
                    rhs, rhs_scale = w_codes[:, g, :], w_scales[:, g, :]
                else:
                    outputs = slice((d - 1) * OUTPUTS, d * OUTPUTS)
                    rhs, rhs_scale = c_codes[:, g, outputs], c_scales[:, g, outputs]
                nc.tensor.matmul_mx(
                    out=acc[:],
                    lhsT=codes[:, rows].bitcast(FP8X4),
                    lhsT_scale=scales[:, rows],
                    rhs=rhs.bitcast(FP8X4),
                    rhs_scale=rhs_scale,
                    start=(opens and local == 0),
                    stop=(closes and local == CHUNK_PASSES - 1),
                )

        def make_offset_rows():
            nc.vector.tensor_tensor(out=offset_rows[:], in0=c0_sum[:], in1=gain_rows[:], op=ALU.mult)
            nc.vector.tensor_tensor(out=offset_rows[:], in0=offset_rows[:], in1=bias_rows[:], op=ALU.add)

        def finish_rows(row_tile):
            shifted = result.tile([P, OUTPUTS], F32, name="shifted", tag="shifted")
            nc.vector.tensor_tensor(out=shifted[:], in0=base_acc[row_tile][:], in1=offset_rows[:], op=ALU.add)
            scaled = result.tile([P, OUTPUTS], F32, name="scaled", tag="scaled")
            nc.vector.tensor_tensor(out=scaled[:], in0=poly_acc[row_tile][:], in1=gain_rows[:], op=ALU.mult)
            total = result.tile([P, OUTPUTS], F32, name="total", tag="total")
            nc.vector.tensor_tensor(out=total[:], in0=scaled[:], in1=shifted[:], op=ALU.add)
            nc.sync.dma_start(out=out[row_tile * P : (row_tile + 1) * P, :], in_=total[:])

        make_identity(nc, identity[:])
        nc.vector.tensor_scalar(out=ones[:], in0=identity[:], scalar1=0.0, scalar2=1.0, op0=ALU.mult, op1=ALU.add)
        load_x(0)
        load_x(1)
        load_c(0)
        load_w()
        load_c(1)
        load_c(2)

        for s in range(-1, CHUNKS + 2):
            transpose_x(s + 1)
            tanh_of_x(s)
            degree_2(s - 1)
            degree_3(s - 1)
            quantise(s - 1, 2)
            if s > CHUNKS_PER_ROW_TILE and s % CHUNKS_PER_ROW_TILE == 1:
                finish_rows((s - 1) // CHUNKS_PER_ROW_TILE - 1)
            regroup_c_pair(s)
            square_t2(s - 1)
            degree_1(s)
            quantise(s - 1, 3)
            quantise_c_pair(s)
            copy_x(s + 1)
            degree_4(s - 1)
            quantise(s, 1)
            square_twice_t(s)
            quantise(s + 1, 0)
            quantise(s - 1, 4)
            if s == CHUNKS_PER_ROW_TILE - 1:
                nc.sync.dma_start(out=gain_rows[:], in_=s1.partition_broadcast(P))
                nc.sync.dma_start(out=bias_rows[:], in_=b1_base.partition_broadcast(P))
            if s == CHUNKS_PER_ROW_TILE:
                make_offset_rows()
            multiply(s - 1, 2)
            multiply(s - 1, 3)
            multiply(s, 1)
            multiply(s + 1, 0)
            multiply(s - 1, 4)
            load_x(s + X_LOADS_AHEAD)
